import numpy as np
import ml_dtypes

BF16 = ml_dtypes.bfloat16


def bf(x):
    return np.asarray(x, np.float32).astype(BF16)


def f32(x):
    return np.asarray(x, np.float32)


def f64(x):
    return np.asarray(x).astype(np.float64)


def striped(idx):
    return np.tile(idx.reshape(-1, 16).T, (8, 1))


C, S, N = 1024, 256, 1024


def setup_inputs():
    return {"weight": f32(np.random.uniform(-1.0, 1.0, (C, S))), "offs": striped(np.concatenate([np.random.permutation(S) for _ in range(-(-(N) // S))])[:N])}


def reference(weight, offs):
    idx = offs[:16].T.reshape(-1)
    return f64(weight)[:, idx]

@@ -1,0 +1,52 @@
+import concourse.mybir as mybir
+
+F32 = mybir.dt.float32
+U16 = mybir.dt.uint16
+COPY = mybir.ActivationFunctionType.Copy
+
+P = 128
+PER_COLUMN = 16
+
+
+def tile_embedding2d_kernel(tc, weight, offs, out):
+    nc = tc.nc
+    channels, codes = weight.shape
+    places = out.shape[1]
+    blocks = channels // P
+    piece = codes
+    pieces = places // piece
+    piece_columns = piece // PER_COLUMN
+
+    with (
+        tc.tile_pool(name="held", bufs=1) as held,
+        tc.tile_pool(name="results", bufs=blocks) as results,
+    ):
+        offsets = held.tile([P, places // PER_COLUMN], U16, name="offsets")
+
+        tables = []
+        for b in range(blocks):
+            table = held.tile([P, codes], F32, name=f"table{b}")
+            nc.sync.dma_start(table[:], weight[b * P : (b + 1) * P, :])
+            tables.append(table)
+            if b == 0:
+                nc.sync.dma_start(offsets[:], offs)
+
+        warm = held.tile([P, 8], F32, name="warm")
+        nc.vector.memset(warm[:], 0.0)
+        nc.scalar.activation(warm[:], warm[:], COPY)
+
+        for b in range(blocks):
+            rows = slice(b * P, (b + 1) * P)
+            last_block = b == blocks - 1
+            picked = results.tile([P, places], F32, name="picked")
+            for k in range(pieces):
+                columns = slice(k * piece, (k + 1) * piece)
+                nc.scalar.activation(
+                    picked[:, columns],
+                    tables[b][:].indirect(offsets[:, k * piece_columns : (k + 1) * piece_columns]),
+                    COPY,
+                )
+                if last_block:
+                    nc.sync.dma_start(out[rows, columns], picked[:, columns])
+            if not last_block:
+                nc.sync.dma_start(out[rows, :], picked[:])

@@ -19,7 +19,8 @@ def tile_embedding2d_kernel(tc, weight, offs, out):
 
     with (
         tc.tile_pool(name="held", bufs=1) as held,
-        tc.tile_pool(name="results", bufs=blocks) as results,
+        tc.tile_pool(name="pairs", bufs=blocks // 4) as pairs,
+        tc.tile_pool(name="results", bufs=blocks // 2) as results,
     ):
         offsets = held.tile([P, places // PER_COLUMN], U16, name="offsets")
 
@@ -35,9 +36,21 @@ def tile_embedding2d_kernel(tc, weight, offs, out):
         nc.vector.memset(warm[:], 0.0)
         nc.scalar.activation(warm[:], warm[:], COPY)
 
-        for b in range(blocks):
+        for b in range(0, blocks // 2, 2):
+            pair = pairs.tile([P, 2, places], F32, name="pair")
+            for t in range(2):
+                for k in range(pieces):
+                    columns = slice(k * piece, (k + 1) * piece)
+                    nc.scalar.activation(
+                        pair[:, t, columns],
+                        tables[b + t][:].indirect(offsets[:, k * piece_columns : (k + 1) * piece_columns]),
+                        COPY,
+                    )
+            both = out[b * P : (b + 2) * P, :].rearrange("(t p) n -> p t n", p=P)
+            nc.sync.dma_start(both, pair[:])
+
+        for b in range(blocks // 2, blocks):
             rows = slice(b * P, (b + 1) * P)
-            last_block = b == blocks - 1
             picked = results.tile([P, places], F32, name="picked")
             for k in range(pieces):
                 columns = slice(k * piece, (k + 1) * piece)
@@ -46,7 +59,8 @@ def tile_embedding2d_kernel(tc, weight, offs, out):
                     tables[b][:].indirect(offsets[:, k * piece_columns : (k + 1) * piece_columns]),
                     COPY,
                 )
-                if last_block:
-                    nc.sync.dma_start(out[rows, columns], picked[:, columns])
-            if not last_block:
-                nc.sync.dma_start(out[rows, :], picked[:])
+                if b == blocks - 1 and k == pieces - 2:
+                    done = columns.stop
+                    nc.sync.dma_start(out[rows, :done], picked[:, :done])
+            left = done if b == blocks - 1 else 0
+            nc.sync.dma_start(out[rows, left:], picked[:, left:])

@@ -19,8 +19,8 @@ def tile_embedding2d_kernel(tc, weight, offs, out):
 
     with (
         tc.tile_pool(name="held", bufs=1) as held,
-        tc.tile_pool(name="pairs", bufs=blocks // 4) as pairs,
-        tc.tile_pool(name="results", bufs=blocks // 2) as results,
+        tc.tile_pool(name="pairs", bufs=blocks // 2 - 1) as pairs,
+        tc.tile_pool(name="results", bufs=2) as results,
     ):
         offsets = held.tile([P, places // PER_COLUMN], U16, name="offsets")
 
@@ -36,7 +36,7 @@ def tile_embedding2d_kernel(tc, weight, offs, out):
         nc.vector.memset(warm[:], 0.0)
         nc.scalar.activation(warm[:], warm[:], COPY)
 
-        for b in range(0, blocks // 2, 2):
+        for b in range(0, blocks - 2, 2):
             pair = pairs.tile([P, 2, places], F32, name="pair")
             for t in range(2):
                 for k in range(pieces):
@@ -49,9 +49,10 @@ def tile_embedding2d_kernel(tc, weight, offs, out):
             both = out[b * P : (b + 2) * P, :].rearrange("(t p) n -> p t n", p=P)
             nc.sync.dma_start(both, pair[:])
 
-        for b in range(blocks // 2, blocks):
+        for b in range(blocks - 2, blocks):
             rows = slice(b * P, (b + 1) * P)
             picked = results.tile([P, places], F32, name="picked")
+            stored = 0
             for k in range(pieces):
                 columns = slice(k * piece, (k + 1) * piece)
                 nc.scalar.activation(
@@ -59,8 +60,6 @@ def tile_embedding2d_kernel(tc, weight, offs, out):
                     tables[b][:].indirect(offsets[:, k * piece_columns : (k + 1) * piece_columns]),
                     COPY,
                 )
-                if b == blocks - 1 and k == pieces - 2:
-                    done = columns.stop
-                    nc.sync.dma_start(out[rows, :done], picked[:, :done])
-            left = done if b == blocks - 1 else 0
-            nc.sync.dma_start(out[rows, left:], picked[:, left:])
+                if k == pieces - 1 or (b == blocks - 1 and k > 0):
+                    nc.sync.dma_start(out[rows, stored : columns.stop], picked[:, stored : columns.stop])
+                    stored = columns.stop

@@ -32,9 +32,8 @@ def tile_embedding2d_kernel(tc, weight, offs, out):
             if b == 0:
                 nc.sync.dma_start(offsets[:], offs)
 
-        warm = held.tile([P, 8], F32, name="warm")
-        nc.vector.memset(warm[:], 0.0)
-        nc.scalar.activation(warm[:], warm[:], COPY)
+        warm = held.tile([P, 8], mybir.dt.uint32, name="warm")
+        nc.scalar.mul(warm[:], warm[:], 0.0)
 
         for b in range(0, blocks - 2, 2):
             pair = pairs.tile([P, 2, places], F32, name="pair")

@@ -19,8 +19,7 @@ def tile_embedding2d_kernel(tc, weight, offs, out):
 
     with (
         tc.tile_pool(name="held", bufs=1) as held,
-        tc.tile_pool(name="pairs", bufs=blocks // 2 - 1) as pairs,
-        tc.tile_pool(name="results", bufs=2) as results,
+        tc.tile_pool(name="results", bufs=1) as results,
     ):
         offsets = held.tile([P, places // PER_COLUMN], U16, name="offsets")
 
@@ -35,30 +34,29 @@ def tile_embedding2d_kernel(tc, weight, offs, out):
         warm = held.tile([P, 8], mybir.dt.uint32, name="warm")
         nc.scalar.mul(warm[:], warm[:], 0.0)
 
-        for b in range(0, blocks - 2, 2):
-            pair = pairs.tile([P, 2, places], F32, name="pair")
-            for t in range(2):
+        first = 0
+        while blocks - first > 1:
+            count = (blocks - first) // 2
+            group = results.tile([P, count, places], F32, name=f"group{first}")
+            for t in range(count):
                 for k in range(pieces):
                     columns = slice(k * piece, (k + 1) * piece)
                     nc.scalar.activation(
-                        pair[:, t, columns],
-                        tables[b + t][:].indirect(offsets[:, k * piece_columns : (k + 1) * piece_columns]),
+                        group[:, t, columns],
+                        tables[first + t][:].indirect(offsets[:, k * piece_columns : (k + 1) * piece_columns]),
                         COPY,
                     )
-            both = out[b * P : (b + 2) * P, :].rearrange("(t p) n -> p t n", p=P)
-            nc.sync.dma_start(both, pair[:])
+            rows = slice(first * P, (first + count) * P)
+            nc.sync.dma_start(out[rows, :].rearrange("(t p) n -> p t n", p=P), group[:])
+            first += count
 
-        for b in range(blocks - 2, blocks):
-            rows = slice(b * P, (b + 1) * P)
-            picked = results.tile([P, places], F32, name="picked")
-            stored = 0
-            for k in range(pieces):
-                columns = slice(k * piece, (k + 1) * piece)
-                nc.scalar.activation(
-                    picked[:, columns],
-                    tables[b][:].indirect(offsets[:, k * piece_columns : (k + 1) * piece_columns]),
-                    COPY,
-                )
-                if k == pieces - 1 or (b == blocks - 1 and k > 0):
-                    nc.sync.dma_start(out[rows, stored : columns.stop], picked[:, stored : columns.stop])
-                    stored = columns.stop
+        rows = slice(first * P, (first + 1) * P)
+        last = results.tile([P, places], F32, name="last")
+        for k in range(pieces):
+            columns = slice(k * piece, (k + 1) * piece)
+            nc.scalar.activation(
+                last[:, columns],
+                tables[first][:].indirect(offsets[:, k * piece_columns : (k + 1) * piece_columns]),
+                COPY,
+            )
+            nc.sync.dma_start(out[rows, columns], last[:, columns])

import concourse.mybir as mybir

F32 = mybir.dt.float32
U16 = mybir.dt.uint16
COPY = mybir.ActivationFunctionType.Copy

P = 128
PER_COLUMN = 16


def tile_embedding2d_kernel(tc, weight, offs, out):
    nc = tc.nc
    channels, codes = weight.shape
    places = out.shape[1]
    blocks = channels // P
    piece = codes
    pieces = places // piece
    piece_columns = piece // PER_COLUMN

    with (
        tc.tile_pool(name="held", bufs=1) as held,
        tc.tile_pool(name="results", bufs=1) as results,
    ):
        offsets = held.tile([P, places // PER_COLUMN], U16, name="offsets")

        tables = []
        for b in range(blocks):
            table = held.tile([P, codes], F32, name=f"table{b}")
            nc.sync.dma_start(table[:], weight[b * P : (b + 1) * P, :])
            tables.append(table)
            if b == 0:
                nc.sync.dma_start(offsets[:], offs)

        warm = held.tile([P, 8], mybir.dt.uint32, name="warm")
        nc.scalar.mul(warm[:], warm[:], 0.0)

        first = 0
        while blocks - first > 1:
            count = (blocks - first) // 2
            group = results.tile([P, count, places], F32, name=f"group{first}")
            for t in range(count):
                for k in range(pieces):
                    columns = slice(k * piece, (k + 1) * piece)
                    nc.scalar.activation(
                        group[:, t, columns],
                        tables[first + t][:].indirect(offsets[:, k * piece_columns : (k + 1) * piece_columns]),
                        COPY,
                    )
            rows = slice(first * P, (first + count) * P)
            nc.sync.dma_start(out[rows, :].rearrange("(t p) n -> p t n", p=P), group[:])
            first += count

        rows = slice(first * P, (first + 1) * P)
        last = results.tile([P, places], F32, name="last")
        for k in range(pieces):
            columns = slice(k * piece, (k + 1) * piece)
            nc.scalar.activation(
                last[:, columns],
                tables[first][:].indirect(offsets[:, k * piece_columns : (k + 1) * piece_columns]),
                COPY,
            )
            nc.sync.dma_start(out[rows, columns], last[:, columns])
